import numpy as np
import ml_dtypes


def mxq(x, axis, fmt="e4m3"):
    dtype, down = {"e4m3": (ml_dtypes.float8_e4m3fn, 7), "e5m2": (ml_dtypes.float8_e5m2, 14)}[fmt]
    v = np.moveaxis(np.asarray(x, np.float32).astype(ml_dtypes.bfloat16).astype(np.float64), axis, -1)
    blocks = v.reshape(v.shape[:-1] + (-1, 32))
    amax = np.abs(blocks).max(-1, keepdims=True)
    byte = np.maximum(np.where(amax > 0, np.frexp(amax)[1] - 1 + 127, 0) - down, 1)
    scale = np.exp2(byte - 127.0)
    codes = (blocks / scale).astype(np.float32).astype(dtype).astype(np.float64)
    return np.moveaxis((codes * scale).reshape(v.shape), -1, axis)


WIDE = False


def mx_kscale(k):
    if not WIDE:
        return np.ones(k)
    levels = np.array([10, -10, 5, -5, 0])
    a = np.random.permutation(np.resize(levels, k // 512 * 4)).reshape(k // 512, 4)
    idx = np.arange(k)
    return np.exp2(a[idx // 512, idx % 128 // 32])


BF16 = ml_dtypes.bfloat16


def bf(x):
    return np.asarray(x, np.float32).astype(BF16)


def f64(x):
    return np.asarray(x).astype(np.float64)


E2M1 = np.array([0.0, 0.5, 1.0, 1.5, 2.0, 3.0, 4.0, 6.0, -0.0, -0.5, -1.0, -1.5, -2.0, -3.0, -4.0, -6.0])


def pack_weight(w, fmt):
    k, n = w.shape
    w = f64(bf(w)).reshape(k // 32, 32, n)
    amax = np.abs(w).max(1)
    if fmt == "e4m3":
        byte = np.frexp(amax)[1] - 1 + 127 - 7
    else:
        mant, ex = np.frexp(amax / 6.0)
        byte = np.where(mant > 0.5, ex, ex - 1) + 127
    byte = np.clip(np.where(amax > 0, byte, 1), 1, 254)
    scaled = (w * np.exp2(127.0 - byte)[:, None, :]).reshape(k, n).astype(np.float32)
    by_word = np.ascontiguousarray(scaled.reshape(k // 512, 128, 4, n).transpose(0, 1, 3, 2))
    if fmt == "e4m3":
        words = by_word.astype(ml_dtypes.float8_e4m3fn).view(np.uint8)
    else:
        c = by_word.astype(ml_dtypes.float4_e2m1fn).view(np.uint8) & 0xF
        words = c[..., 0::2] | (c[..., 1::2] << 4)
    return np.ascontiguousarray(words), np.ascontiguousarray(byte.astype(np.uint8).reshape(k // 512, 16, n))


def unpack_weight(words, scales, fmt):
    g, p, n, _ = words.shape
    if fmt == "e4m3":
        vals = np.ascontiguousarray(words).view(ml_dtypes.float8_e4m3fn).astype(np.float64)
    else:
        nib = np.empty((g, p, n, 4), np.uint8)
        nib[..., 0::2] = words & 0xF
        nib[..., 1::2] = words >> 4
        vals = E2M1[nib]
    vals = vals * np.repeat(np.exp2(scales.astype(np.float64) - 127.0), 8, axis=1)[..., None]
    return vals.transpose(0, 1, 3, 2).reshape(g * 512, n)


B, P, D, DFF = 2, 64, 512, 2048


def sigmoid(v):
    return 1.0 / (1.0 + np.exp(-v))


def setup_inputs():
    s = mx_kscale(D)
    inp = {
        'Zi': bf(np.random.standard_normal((B, P, D)) * s),
        'Ci': bf(np.random.standard_normal((B, P, DFF))),
        'Mi': bf(np.random.standard_normal((B, P, DFF))),
        'Hi': bf(np.random.standard_normal((B, P, DFF))),
        'Ni': bf(np.random.uniform(0.5, 1.5, (B, P, DFF))),
        'm': bf(np.random.uniform(0.0, 1.0, (B, P, 1))),
    }
    for n in ('WI', 'WF', 'WO', 'WZ'):
        words, scales = pack_weight(np.random.standard_normal((DFF, DFF)) * 0.7 / np.sqrt(DFF), 'e4m3')
        inp[n + '_w_words'] = words
        inp[n + '_w_scales'] = scales
        inp[n + '_b'] = bf(np.random.standard_normal(DFF) * 0.3)
    for n in ('RI', 'RF', 'RO', 'RZ'):
        words, scales = pack_weight(np.random.standard_normal((D, DFF)) * 0.7 / np.sqrt(D) / s[:, None], 'e4m3')
        inp[n + '_w_words'] = words
        inp[n + '_w_scales'] = scales
        inp[n + '_b'] = bf(np.random.standard_normal(DFF) * 0.3)
    return inp


def reference(Zi, Ci, Mi, Hi, Ni, m,
              WI_w_words, WI_w_scales, WI_b, WF_w_words, WF_w_scales, WF_b,
              WO_w_words, WO_w_scales, WO_b, WZ_w_words, WZ_w_scales, WZ_b,
              RI_w_words, RI_w_scales, RI_b, RF_w_words, RF_w_scales, RF_b,
              RO_w_words, RO_w_scales, RO_b, RZ_w_words, RZ_w_scales, RZ_b):
    Zi, Ci, Mi, Hi, Ni, m = f64(Zi), f64(Ci), f64(Mi), f64(Hi), f64(Ni), f64(m)
    Wh = np.concatenate([unpack_weight(WI_w_words, WI_w_scales, 'e4m3'), unpack_weight(WF_w_words, WF_w_scales, 'e4m3'),
                         unpack_weight(WO_w_words, WO_w_scales, 'e4m3'), unpack_weight(WZ_w_words, WZ_w_scales, 'e4m3')], axis=1)
    Wz = np.concatenate([unpack_weight(RI_w_words, RI_w_scales, 'e4m3'), unpack_weight(RF_w_words, RF_w_scales, 'e4m3'),
                         unpack_weight(RO_w_words, RO_w_scales, 'e4m3'), unpack_weight(RZ_w_words, RZ_w_scales, 'e4m3')], axis=1)
    bias = np.concatenate([f64(WI_b) + f64(RI_b), f64(WF_b) + f64(RF_b), f64(WO_b) + f64(RO_b), f64(WZ_b) + f64(RZ_b)])
    gates = (mxq(Hi, 2, 'e4m3') @ Wh) + (mxq(Zi, 2, 'e4m3') @ Wz) + bias
    I_tilde, F_tilde, O_tilde, Z_tilde = np.split(gates, 4, axis=-1)

    M_t = np.maximum(F_tilde + Mi, I_tilde)
    I_t = np.exp(I_tilde - M_t)
    F_t = np.exp(F_tilde + Mi - M_t)
    O_t = sigmoid(O_tilde)
    N_t = F_t * Ni + I_t
    Z_t = np.tanh(Z_tilde)
    C_t = (Ci * F_t + Z_t * I_t) * m + (1.0 - m) * Ci
    H_t = O_t * (C_t / N_t) * m + (1.0 - m) * Hi
    return (C_t, M_t, H_t, N_t)

@@ -1,0 +1,315 @@
+from contextlib import ExitStack
+
+import concourse.mybir as mybir
+from concourse.masks import make_identity
+
+F32 = mybir.dt.float32
+BF16 = mybir.dt.bfloat16
+I32 = mybir.dt.int32
+U32 = mybir.dt.uint32
+U8 = mybir.dt.uint8
+FP8X4 = mybir.dt.float8_e4m3fn_x4
+ALU = mybir.AluOpType
+ACT = mybir.ActivationFunctionType
+
+P = 128
+D_H = 2048
+D_Z = 512
+K_PASS = 512
+H_GROUPS = D_H // K_PASS
+GROUPS = H_GROUPS + D_Z // K_PASS
+BANK = 512
+CHUNKS = D_H // BANK
+QUADRANTS = 4
+GATE_I, GATE_F, GATE_Z, GATE_O = 0, 1, 2, 3
+RING = 6
+SMALL_PER_TILE = 4
+LAG = 2
+
+FLOPS = 2 * P * (D_H + D_Z) * 4 * D_H
+
+
+def tile_customlstmcell_w_kernel(
+    tc, Zi, Ci, Mi, Hi, Ni, m,
+    WI_w_words, WI_w_scales, WI_b, WF_w_words, WF_w_scales, WF_b,
+    WO_w_words, WO_w_scales, WO_b, WZ_w_words, WZ_w_scales, WZ_b,
+    RI_w_words, RI_w_scales, RI_b, RF_w_words, RF_w_scales, RF_b,
+    RO_w_words, RO_w_scales, RO_b, RZ_w_words, RZ_w_scales, RZ_b,
+    out_0, out_1, out_2, out_3,
+):
+    nc = tc.nc
+    w_words = [WI_w_words, WF_w_words, WZ_w_words, WO_w_words]
+    w_scales = [WI_w_scales, WF_w_scales, WZ_w_scales, WO_w_scales]
+    w_bias = [WI_b, WF_b, WZ_b, WO_b]
+    r_words = [RI_w_words, RF_w_words, RZ_w_words, RO_w_words]
+    r_scales = [RI_w_scales, RF_w_scales, RZ_w_scales, RO_w_scales]
+    r_bias = [RI_b, RF_b, RZ_b, RO_b]
+    c_out, m_out, h_out, n_out = [o.flatten_outer_dims() for o in (out_0, out_1, out_2, out_3)]
+
+    late_tiles = [(gate, c) for gate in (GATE_Z, GATE_O) for c in range(CHUNKS)]
+    tile_order = [(gate, c) for c in range(CHUNKS) for gate in (GATE_I, GATE_F)] + late_tiles
+
+    def cols(c):
+        return slice(BANK * c, BANK * (c + 1))
+
+    with ExitStack() as stack:
+        const = stack.enter_context(tc.tile_pool(name="const", bufs=1))
+        ring = stack.enter_context(tc.tile_pool(name="ring", bufs=RING))
+        work = stack.enter_context(tc.tile_pool(name="work", bufs=2))
+        late = stack.enter_context(tc.tile_pool(name="late", bufs=LAG + 1))
+        psum = stack.enter_context(tc.psum_pool(name="psum", bufs=8))
+        stack.enter_context(tc.manual_schedule())
+
+        ident_f32 = const.tile([P, P], F32)
+        make_identity(nc, ident_f32[:])
+
+        planes = const.tile([P, 5, D_H], U8, align_bytes=64)
+        nc.vector.memset(planes[:].bitcast(I32), 0)
+
+        bias_rows = const.tile([P, D_H], BF16)
+        nc.vector.memset(bias_rows[:], 0.0)
+        selector = const.tile([P, 4, P], BF16)
+        nc.vector.memset(selector[:], 0.0)
+        for gate in range(4):
+            nc.vector.memset(selector[32 * gate : 32 * gate + 32, gate, :], 1.0)
+
+        hi_sb = const.tile([P, D_H], BF16)
+        zi_sb = const.tile([P, D_Z], BF16)
+        mi_sb = const.tile([P, D_H], BF16)
+        ni_sb = const.tile([P, D_H], BF16)
+        ci_sb = const.tile([P, D_H], BF16)
+        m_bf16 = const.tile([P, 1], BF16)
+
+        def scale_plane_loads(gate):
+            pairs = []
+            for quad in range(QUADRANTS):
+                rows = slice(4 * quad, 4 * quad + 4)
+                first = 32 * quad
+                pairs.append((
+                    planes[first : first + 16, gate, :].bitcast(I32),
+                    w_scales[gate][:, rows, :].bitcast(I32),
+                ))
+                pairs.append((
+                    planes[first + 4 * gate : first + 4 * gate + 4, 4, :].bitcast(I32),
+                    r_scales[gate][0, rows, :].bitcast(I32),
+                ))
+            return pairs
+
+        def bias_row_loads(gate):
+            return [
+                (bias_rows[row : row + 1, :], vector.rearrange("(o n) -> o n", o=1))
+                for row, vector in ((32 * gate, w_bias[gate]), (32 * gate + 1, r_bias[gate]))
+            ]
+
+        def load(pairs):
+            for destination, source in pairs:
+                nc.sync.dma_start(out=destination, in_=source)
+
+        waiting = (
+            bias_row_loads(GATE_Z)
+            + bias_row_loads(GATE_O)
+            + [(ni_sb[:], Ni.flatten_outer_dims()), (ci_sb[:], Ci.flatten_outer_dims())]
+            + scale_plane_loads(GATE_Z)
+            + scale_plane_loads(GATE_O)
+        )
+        weight_tiles = {}
+
+        def load_weight_tile(index):
+            gate, c = tile_order[index]
+            byte_cols = slice(4 * BANK * c, 4 * BANK * (c + 1))
+            words = ring.tile([P, GROUPS, BANK], I32, tag="words", align_bytes=64)
+            nc.sync.dma_start(
+                out=words[:, 0:H_GROUPS, :],
+                in_=w_words[gate].rearrange("g p n t -> p g (n t)")[:, :, byte_cols].bitcast(I32),
+            )
+            nc.sync.dma_start(
+                out=words[:, H_GROUPS, :],
+                in_=r_words[gate].rearrange("g p n t -> p g (n t)")[:, 0, byte_cols].bitcast(I32),
+            )
+            weight_tiles[(gate, c)] = words
+            if index >= 2:
+                load(waiting[SMALL_PER_TILE * (index - 2) : SMALL_PER_TILE * (index - 1)])
+
+        load([(hi_sb[:], Hi.flatten_outer_dims()), (zi_sb[:], Zi.flatten_outer_dims())])
+        load_weight_tile(0)
+        load(scale_plane_loads(GATE_I))
+        load([(m_bf16[:], m.flatten_outer_dims())] + bias_row_loads(GATE_I) + bias_row_loads(GATE_F))
+        load_weight_tile(1)
+        load([(mi_sb[:], Mi.flatten_outer_dims())])
+        load(scale_plane_loads(GATE_F))
+        for index in range(2, RING):
+            load_weight_tile(index)
+
+        m_f32 = const.tile([P, 1], F32)
+        nc.vector.tensor_copy(out=m_f32[:], in_=m_bf16[:])
+        one_minus_m = const.tile([P, 1], F32)
+        nc.vector.tensor_scalar(
+            out=one_minus_m[:], in0=m_bf16[:], scalar1=-1.0, scalar2=1.0, op0=ALU.mult, op1=ALU.add
+        )
+
+        x_bf16 = const.tile([P, GROUPS, P, 4], BF16, align_bytes=64)
+        x_codes = const.tile([P, GROUPS, P], U32, align_bytes=64)
+        x_scales = const.tile([P, GROUPS, P], U8, align_bytes=64)
+
+        def transpose_groups(source, first_group, n_groups):
+            source_words = source.bitcast(F32)
+            halves = psum.tile([P, n_groups, 2, P], F32, tag="bank")
+            for g in range(n_groups):
+                for u in range(2):
+                    nc.tensor.transpose(
+                        halves[:, g, u, :],
+                        source_words[:, 256 * g + u : 256 * (g + 1) : 2],
+                        ident_f32[:],
+                    )
+            nc.vector.tensor_copy(
+                out=x_bf16[:, first_group : first_group + n_groups].bitcast(F32),
+                in_=halves[:].rearrange("p g u r -> p g r u"),
+            )
+
+        def quantise_groups(first_group, n_groups):
+            groups = slice(first_group, first_group + n_groups)
+            nc.vector.quantize_mx(
+                out=x_codes[:, groups, :].rearrange("p g r -> p (g r)").bitcast(FP8X4),
+                scales=x_scales[:, groups, :].rearrange("p g r -> p (g r)"),
+                in_=x_bf16[:, groups].rearrange("p g r t -> p (g r t)"),
+            )
+
+        transpose_groups(hi_sb[:, 0 : 2 * K_PASS], 0, 2)
+        transpose_groups(hi_sb[:, 2 * K_PASS : 4 * K_PASS], 2, 2)
+        transpose_groups(zi_sb[:], H_GROUPS, 1)
+        quantise_groups(0, H_GROUPS)
+        quantise_groups(H_GROUPS, 1)
+
+        bias = [const.tile([P, D_H], F32, name="bias%d" % gate) for gate in range(4)]
+
+        def broadcast_bias(gate, c):
+            bank = psum.tile([P, BANK], F32, tag="bank")
+            nc.tensor.matmul(
+                out=bank[:], lhsT=selector[:, gate, :], rhs=bias_rows[:, cols(c)], start=True, stop=True
+            )
+            if gate == GATE_F:
+                nc.vector.tensor_tensor(
+                    out=bias[gate][:, cols(c)], in0=bank[:], in1=mi_sb[:, cols(c)], op=ALU.add
+                )
+            else:
+                nc.scalar.copy(out=bias[gate][:, cols(c)], in_=bank[:])
+
+        for c in range(CHUNKS):
+            broadcast_bias(GATE_I, c)
+            broadcast_bias(GATE_F, c)
+
+        m_all = const.tile([P, D_H], F32)
+        n_all = const.tile([P, D_H], F32)
+        c_all = const.tile([P, D_H], F32)
+        h_all = const.tile([P, D_H], F32)
+        i_all = const.tile([P, D_H], F32)
+        keep_all = const.tile([P, D_H], F32)
+        inv_n_sq = const.tile([P, D_H], F32)
+        c_times_n = const.tile([P, D_H], F32)
+        c_over_n = const.tile([P, D_H], F32)
+
+        def preactivation(gate, c, pool, tag):
+            words = weight_tiles[(gate, c)]
+            acc = psum.tile([P, BANK], F32, tag="bank")
+            for g in range(GROUPS):
+                if g < H_GROUPS:
+                    plane = planes[4 * g : P, gate, cols(c)]
+                else:
+                    plane = planes[4 * gate : P, 4, cols(c)]
+                nc.tensor.matmul_mx(
+                    out=acc[:],
+                    lhsT=x_codes[:, g, :].bitcast(FP8X4),
+                    lhsT_scale=x_scales[:, g, :],
+                    rhs=words[:, g, :].bitcast(FP8X4),
+                    rhs_scale=plane,
+                    start=(g == 0),
+                    stop=(g == GROUPS - 1),
+                )
+            follower = tile_order.index((gate, c)) + RING
+            if follower < len(tile_order):
+                load_weight_tile(follower)
+            pre = pool.tile([P, BANK], F32, tag=tag)
+            nc.vector.tensor_tensor(out=pre[:], in0=acc[:], in1=bias[gate][:, cols(c)], op=ALU.add)
+            return pre
+
+        def input_and_forget(c):
+            g_i = preactivation(GATE_I, c, work, "g_i")
+            g_f = preactivation(GATE_F, c, work, "g_f")
+            diff = work.tile([P, BANK], F32, tag="diff")
+            nc.vector.tensor_tensor(out=diff[:], in0=g_f[:], in1=g_i[:], op=ALU.subtract)
+            nc.vector.tensor_tensor(out=m_all[:, cols(c)], in0=g_f[:], in1=g_i[:], op=ALU.max)
+            f_t = work.tile([P, BANK], F32, tag="f_t")
+            nc.scalar.activation(out=f_t[:], in_=diff[:], func=ACT.Relu, scale=-1.0)
+            nc.scalar.activation(out=f_t[:], in_=f_t[:], func=ACT.Exp, scale=-1.0)
+            nc.scalar.activation(out=i_all[:, cols(c)], in_=diff[:], func=ACT.Relu)
+            nc.scalar.activation(out=i_all[:, cols(c)], in_=i_all[:, cols(c)], func=ACT.Exp, scale=-1.0)
+            nc.scalar.activation(
+                out=keep_all[:, cols(c)], in_=f_t[:], func=ACT.Identity,
+                scale=m_f32[:], bias=one_minus_m[:],
+            )
+            return f_t
+
+        def normaliser(c, f_t):
+            n_t = n_all[:, cols(c)]
+            nc.vector.tensor_tensor(out=n_t, in0=f_t[:], in1=ni_sb[:, cols(c)], op=ALU.mult)
+            nc.vector.tensor_tensor(out=n_t, in0=n_t, in1=i_all[:, cols(c)], op=ALU.add)
+            nc.scalar.activation(out=inv_n_sq[:, cols(c)], in_=n_t, func=ACT.Abs)
+            nc.vector.tensor_tensor(
+                out=keep_all[:, cols(c)], in0=keep_all[:, cols(c)], in1=ci_sb[:, cols(c)], op=ALU.mult
+            )
+
+        def cell(c, z_t):
+            c_t = c_all[:, cols(c)]
+            nc.vector.scalar_tensor_tensor(
+                out=c_t, in0=z_t[:], scalar=m_f32[:], in1=i_all[:, cols(c)], op0=ALU.mult, op1=ALU.mult
+            )
+            nc.vector.tensor_tensor(out=c_t, in0=c_t, in1=keep_all[:, cols(c)], op=ALU.add)
+            nc.vector.tensor_tensor(out=c_times_n[:, cols(c)], in0=c_t, in1=n_all[:, cols(c)], op=ALU.mult)
+
+        def hidden(c, o_t):
+            h_t = h_all[:, cols(c)]
+            nc.vector.scalar_tensor_tensor(
+                out=h_t, in0=o_t[:], scalar=m_f32[:], in1=c_over_n[:, cols(c)], op0=ALU.mult, op1=ALU.mult
+            )
+            nc.vector.scalar_tensor_tensor(
+                out=h_t, in0=hi_sb[:, cols(c)], scalar=one_minus_m[:], in1=h_t, op0=ALU.mult, op1=ALU.add
+            )
+            nc.sync.dma_start(out=h_out[:, cols(c)], in_=h_t)
+
+        f_ts = {}
+        for c in range(CHUNKS):
+            f_ts[c] = input_and_forget(c)
+            if c > 0:
+                normaliser(c - 1, f_ts[c - 1])
+            broadcast_bias(GATE_Z, c)
+            broadcast_bias(GATE_O, c)
+
+        def finish(step):
+            gate, c = late_tiles[step]
+            if gate == GATE_Z:
+                cell(c, activated[step])
+            else:
+                hidden(c, activated[step])
+
+        activated = {}
+        for step, (gate, c) in enumerate(late_tiles):
+            activated[step] = preactivation(gate, c, late, "late")
+            if step == 0:
+                normaliser(CHUNKS - 1, f_ts[CHUNKS - 1])
+            nc.scalar.activation(
+                out=activated[step][:], in_=activated[step][:],
+                func=(ACT.Tanh if gate == GATE_Z else ACT.Sigmoid),
+            )
+            if (gate, c) == (GATE_Z, CHUNKS - 2):
+                nc.scalar.activation(out=inv_n_sq[:], in_=inv_n_sq[:], func=ACT.Ln)
+            if (gate, c) == (GATE_Z, CHUNKS - 1):
+                nc.scalar.activation(out=inv_n_sq[:], in_=inv_n_sq[:], func=ACT.Exp, scale=-2.0)
+                nc.sync.dma_start(out=m_out, in_=m_all[:])
+                nc.sync.dma_start(out=n_out, in_=n_all[:])
+            if step >= LAG:
+                finish(step - LAG)
+            if step - LAG == CHUNKS - 1:
+                nc.sync.dma_start(out=c_out, in_=c_all[:])
+                nc.vector.tensor_tensor(out=c_over_n[:], in0=c_times_n[:], in1=inv_n_sq[:], op=ALU.mult)
+        for step in range(len(late_tiles) - LAG, len(late_tiles)):
+            finish(step)

@@ -63,15 +63,18 @@ def tile_customlstmcell_w_kernel(
         ident_f32 = const.tile([P, P], F32)
         make_identity(nc, ident_f32[:])
 
-        planes = const.tile([P, 5, D_H], U8, align_bytes=64)
-        nc.vector.memset(planes[:].bitcast(I32), 0)
+        h_planes = const.tile([P, 4, D_H], U8, align_bytes=64)
+        nc.vector.memset(h_planes[:].bitcast(I32), 0)
+        z_planes = const.tile([P, 4, BANK], U8, align_bytes=64)
+        nc.vector.memset(z_planes[:].bitcast(I32), 0)
 
-        bias_rows = const.tile([P, D_H], BF16)
-        nc.vector.memset(bias_rows[:], 0.0)
-        selector = const.tile([P, 4, P], BF16)
+        bias_rows = [const.tile([P, D_H], BF16, name="bias_rows%d" % pair) for pair in range(2)]
+        for pair in range(2):
+            nc.vector.memset(bias_rows[pair][:], 0.0)
+        selector = const.tile([P, 2, P], BF16)
         nc.vector.memset(selector[:], 0.0)
-        for gate in range(4):
-            nc.vector.memset(selector[32 * gate : 32 * gate + 32, gate, :], 1.0)
+        for second in range(2):
+            nc.vector.memset(selector[32 * second : 32 * second + 32, second, :], 1.0)
 
         hi_sb = const.tile([P, D_H], BF16)
         zi_sb = const.tile([P, D_Z], BF16)
@@ -84,21 +87,22 @@ def tile_customlstmcell_w_kernel(
             pairs = []
             for quad in range(QUADRANTS):
                 rows = slice(4 * quad, 4 * quad + 4)
-                first = 32 * quad
+                live = slice(32 * quad, 32 * quad + 16)
                 pairs.append((
-                    planes[first : first + 16, gate, :].bitcast(I32),
+                    h_planes[live, gate, :].bitcast(I32),
                     w_scales[gate][:, rows, :].bitcast(I32),
                 ))
                 pairs.append((
-                    planes[first + 4 * gate : first + 4 * gate + 4, 4, :].bitcast(I32),
-                    r_scales[gate][0, rows, :].bitcast(I32),
+                    z_planes[live, gate, :].bitcast(I32),
+                    r_scales[gate][0, rows, :].rearrange("r (c n) -> c r n", c=CHUNKS).bitcast(I32),
                 ))
             return pairs
 
         def bias_row_loads(gate):
+            first = 32 * (gate % 2)
             return [
-                (bias_rows[row : row + 1, :], vector.rearrange("(o n) -> o n", o=1))
-                for row, vector in ((32 * gate, w_bias[gate]), (32 * gate + 1, r_bias[gate]))
+                (bias_rows[gate // 2][row : row + 1, :], vector.rearrange("(o n) -> o n", o=1))
+                for row, vector in ((first, w_bias[gate]), (first + 1, r_bias[gate]))
             ]
 
         def load(pairs):
@@ -185,7 +189,8 @@ def tile_customlstmcell_w_kernel(
         def broadcast_bias(gate, c):
             bank = psum.tile([P, BANK], F32, tag="bank")
             nc.tensor.matmul(
-                out=bank[:], lhsT=selector[:, gate, :], rhs=bias_rows[:, cols(c)], start=True, stop=True
+                out=bank[:], lhsT=selector[:, gate % 2, :], rhs=bias_rows[gate // 2][:, cols(c)],
+                start=True, stop=True,
             )
             if gate == GATE_F:
                 nc.vector.tensor_tensor(
@@ -202,20 +207,19 @@ def tile_customlstmcell_w_kernel(
         n_all = const.tile([P, D_H], F32)
         c_all = const.tile([P, D_H], F32)
         h_all = const.tile([P, D_H], F32)
-        i_all = const.tile([P, D_H], F32)
+        i_all = const.tile([P, D_H], F32, tag="i_then_c_over_n")
         keep_all = const.tile([P, D_H], F32)
         inv_n_sq = const.tile([P, D_H], F32)
         c_times_n = const.tile([P, D_H], F32)
-        c_over_n = const.tile([P, D_H], F32)
 
         def preactivation(gate, c, pool, tag):
             words = weight_tiles[(gate, c)]
             acc = psum.tile([P, BANK], F32, tag="bank")
             for g in range(GROUPS):
                 if g < H_GROUPS:
-                    plane = planes[4 * g : P, gate, cols(c)]
+                    plane = h_planes[4 * g : P, gate, cols(c)]
                 else:
-                    plane = planes[4 * gate : P, 4, cols(c)]
+                    plane = z_planes[4 * c : P, gate, :]
                 nc.tensor.matmul_mx(
                     out=acc[:],
                     lhsT=x_codes[:, g, :].bitcast(FP8X4),
@@ -310,6 +314,7 @@ def tile_customlstmcell_w_kernel(
                 finish(step - LAG)
             if step - LAG == CHUNKS - 1:
                 nc.sync.dma_start(out=c_out, in_=c_all[:])
+                c_over_n = const.tile([P, D_H], F32, tag="i_then_c_over_n")
                 nc.vector.tensor_tensor(out=c_over_n[:], in0=c_times_n[:], in1=inv_n_sq[:], op=ALU.mult)
         for step in range(len(late_tiles) - LAG, len(late_tiles)):
             finish(step)

@@ -23,7 +23,7 @@ CHUNKS = D_H // BANK
 QUADRANTS = 4
 GATE_I, GATE_F, GATE_Z, GATE_O = 0, 1, 2, 3
 RING = 6
-SMALL_PER_TILE = 4
+SMALL_PER_TILE = 5
 LAG = 2
 
 FLOPS = 2 * P * (D_H + D_Z) * 4 * D_H
@@ -110,7 +110,13 @@ def tile_customlstmcell_w_kernel(
                 nc.sync.dma_start(out=destination, in_=source)
 
         waiting = (
-            bias_row_loads(GATE_Z)
+            scale_plane_loads(GATE_I)
+            + [(m_bf16[:], m.flatten_outer_dims())]
+            + bias_row_loads(GATE_I)
+            + bias_row_loads(GATE_F)
+            + [(mi_sb[:], Mi.flatten_outer_dims())]
+            + scale_plane_loads(GATE_F)
+            + bias_row_loads(GATE_Z)
             + bias_row_loads(GATE_O)
             + [(ni_sb[:], Ni.flatten_outer_dims()), (ci_sb[:], Ci.flatten_outer_dims())]
             + scale_plane_loads(GATE_Z)
@@ -131,17 +137,10 @@ def tile_customlstmcell_w_kernel(
                 in_=r_words[gate].rearrange("g p n t -> p g (n t)")[:, 0, byte_cols].bitcast(I32),
             )
             weight_tiles[(gate, c)] = words
-            if index >= 2:
-                load(waiting[SMALL_PER_TILE * (index - 2) : SMALL_PER_TILE * (index - 1)])
+            load(waiting[SMALL_PER_TILE * index : SMALL_PER_TILE * (index + 1)])
 
         load([(hi_sb[:], Hi.flatten_outer_dims()), (zi_sb[:], Zi.flatten_outer_dims())])
-        load_weight_tile(0)
-        load(scale_plane_loads(GATE_I))
-        load([(m_bf16[:], m.flatten_outer_dims())] + bias_row_loads(GATE_I) + bias_row_loads(GATE_F))
-        load_weight_tile(1)
-        load([(mi_sb[:], Mi.flatten_outer_dims())])
-        load(scale_plane_loads(GATE_F))
-        for index in range(2, RING):
+        for index in range(RING):
             load_weight_tile(index)
 
         m_f32 = const.tile([P, 1], F32)

@@ -20,10 +20,11 @@ H_GROUPS = D_H // K_PASS
 GROUPS = H_GROUPS + D_Z // K_PASS
 BANK = 512
 CHUNKS = D_H // BANK
+PSUM_BANKS = 8
 QUADRANTS = 4
 GATE_I, GATE_F, GATE_Z, GATE_O = 0, 1, 2, 3
 RING = 6
-SMALL_PER_TILE = 5
+SMALL_PER_TILE = 4
 LAG = 2
 
 FLOPS = 2 * P * (D_H + D_Z) * 4 * D_H
@@ -56,8 +57,8 @@ def tile_customlstmcell_w_kernel(
         const = stack.enter_context(tc.tile_pool(name="const", bufs=1))
         ring = stack.enter_context(tc.tile_pool(name="ring", bufs=RING))
         work = stack.enter_context(tc.tile_pool(name="work", bufs=2))
-        late = stack.enter_context(tc.tile_pool(name="late", bufs=LAG + 1))
-        psum = stack.enter_context(tc.psum_pool(name="psum", bufs=8))
+        late = stack.enter_context(tc.tile_pool(name="late", bufs=CHUNKS))
+        psum = stack.enter_context(tc.psum_pool(name="psum", bufs=PSUM_BANKS))
         stack.enter_context(tc.manual_schedule())
 
         ident_f32 = const.tile([P, P], F32)
@@ -84,19 +85,19 @@ def tile_customlstmcell_w_kernel(
         m_bf16 = const.tile([P, 1], BF16)
 
         def scale_plane_loads(gate):
-            pairs = []
+            transfers = []
             for quad in range(QUADRANTS):
                 rows = slice(4 * quad, 4 * quad + 4)
                 live = slice(32 * quad, 32 * quad + 16)
-                pairs.append((
+                transfers.append((
                     h_planes[live, gate, :].bitcast(I32),
                     w_scales[gate][:, rows, :].bitcast(I32),
                 ))
-                pairs.append((
+                transfers.append((
                     z_planes[live, gate, :].bitcast(I32),
                     r_scales[gate][0, rows, :].rearrange("r (c n) -> c r n", c=CHUNKS).bitcast(I32),
                 ))
-            return pairs
+            return transfers
 
         def bias_row_loads(gate):
             first = 32 * (gate % 2)
@@ -105,18 +106,12 @@ def tile_customlstmcell_w_kernel(
                 for row, vector in ((first, w_bias[gate]), (first + 1, r_bias[gate]))
             ]
 
-        def load(pairs):
-            for destination, source in pairs:
+        def load(transfers):
+            for destination, source in transfers:
                 nc.sync.dma_start(out=destination, in_=source)
 
         waiting = (
-            scale_plane_loads(GATE_I)
-            + [(m_bf16[:], m.flatten_outer_dims())]
-            + bias_row_loads(GATE_I)
-            + bias_row_loads(GATE_F)
-            + [(mi_sb[:], Mi.flatten_outer_dims())]
-            + scale_plane_loads(GATE_F)
-            + bias_row_loads(GATE_Z)
+            bias_row_loads(GATE_Z)
             + bias_row_loads(GATE_O)
             + [(ni_sb[:], Ni.flatten_outer_dims()), (ci_sb[:], Ci.flatten_outer_dims())]
             + scale_plane_loads(GATE_Z)
@@ -137,18 +132,18 @@ def tile_customlstmcell_w_kernel(
                 in_=r_words[gate].rearrange("g p n t -> p g (n t)")[:, 0, byte_cols].bitcast(I32),
             )
             weight_tiles[(gate, c)] = words
-            load(waiting[SMALL_PER_TILE * index : SMALL_PER_TILE * (index + 1)])
+            if index >= 2:
+                load(waiting[SMALL_PER_TILE * (index - 2) : SMALL_PER_TILE * (index - 1)])
 
         load([(hi_sb[:], Hi.flatten_outer_dims()), (zi_sb[:], Zi.flatten_outer_dims())])
-        for index in range(RING):
+        load_weight_tile(0)
+        load(scale_plane_loads(GATE_I))
+        load([(m_bf16[:], m.flatten_outer_dims())] + bias_row_loads(GATE_I) + bias_row_loads(GATE_F))
+        load_weight_tile(1)
+        load([(mi_sb[:], Mi.flatten_outer_dims())])
+        load(scale_plane_loads(GATE_F))
+        for index in range(2, RING):
             load_weight_tile(index)
-
-        m_f32 = const.tile([P, 1], F32)
-        nc.vector.tensor_copy(out=m_f32[:], in_=m_bf16[:])
-        one_minus_m = const.tile([P, 1], F32)
-        nc.vector.tensor_scalar(
-            out=one_minus_m[:], in0=m_bf16[:], scalar1=-1.0, scalar2=1.0, op0=ALU.mult, op1=ALU.add
-        )
 
         x_bf16 = const.tile([P, GROUPS, P, 4], BF16, align_bytes=64)
         x_codes = const.tile([P, GROUPS, P], U32, align_bytes=64)
@@ -202,6 +197,13 @@ def tile_customlstmcell_w_kernel(
             broadcast_bias(GATE_I, c)
             broadcast_bias(GATE_F, c)
 
+        m_f32 = const.tile([P, 1], F32)
+        nc.vector.tensor_copy(out=m_f32[:], in_=m_bf16[:])
+        one_minus_m = const.tile([P, 1], F32)
+        nc.vector.tensor_scalar(
+            out=one_minus_m[:], in0=m_bf16[:], scalar1=-1.0, scalar2=1.0, op0=ALU.mult, op1=ALU.add
+        )
+
         m_all = const.tile([P, D_H], F32)
         n_all = const.tile([P, D_H], F32)
         c_all = const.tile([P, D_H], F32)
@@ -235,85 +237,105 @@ def tile_customlstmcell_w_kernel(
             nc.vector.tensor_tensor(out=pre[:], in0=acc[:], in1=bias[gate][:, cols(c)], op=ALU.add)
             return pre
 
-        def input_and_forget(c):
-            g_i = preactivation(GATE_I, c, work, "g_i")
-            g_f = preactivation(GATE_F, c, work, "g_f")
-            diff = work.tile([P, BANK], F32, tag="diff")
-            nc.vector.tensor_tensor(out=diff[:], in0=g_f[:], in1=g_i[:], op=ALU.subtract)
-            nc.vector.tensor_tensor(out=m_all[:, cols(c)], in0=g_f[:], in1=g_i[:], op=ALU.max)
+
+        def gate_exponentials(c, diff):
             f_t = work.tile([P, BANK], F32, tag="f_t")
+            i_t = i_all[:, cols(c)]
             nc.scalar.activation(out=f_t[:], in_=diff[:], func=ACT.Relu, scale=-1.0)
+            nc.scalar.activation(out=i_t, in_=diff[:], func=ACT.Relu)
             nc.scalar.activation(out=f_t[:], in_=f_t[:], func=ACT.Exp, scale=-1.0)
-            nc.scalar.activation(out=i_all[:, cols(c)], in_=diff[:], func=ACT.Relu)
-            nc.scalar.activation(out=i_all[:, cols(c)], in_=i_all[:, cols(c)], func=ACT.Exp, scale=-1.0)
+            nc.scalar.activation(out=i_t, in_=i_t, func=ACT.Exp, scale=-1.0)
             nc.scalar.activation(
                 out=keep_all[:, cols(c)], in_=f_t[:], func=ACT.Identity,
                 scale=m_f32[:], bias=one_minus_m[:],
             )
             return f_t
 
-        def normaliser(c, f_t):
+        def normaliser_product(c, f_t):
+            nc.vector.tensor_tensor(out=n_all[:, cols(c)], in0=f_t[:], in1=ni_sb[:, cols(c)], op=ALU.mult)
+
+        def normaliser_sum(c):
             n_t = n_all[:, cols(c)]
-            nc.vector.tensor_tensor(out=n_t, in0=f_t[:], in1=ni_sb[:, cols(c)], op=ALU.mult)
             nc.vector.tensor_tensor(out=n_t, in0=n_t, in1=i_all[:, cols(c)], op=ALU.add)
             nc.scalar.activation(out=inv_n_sq[:, cols(c)], in_=n_t, func=ACT.Abs)
-            nc.vector.tensor_tensor(
-                out=keep_all[:, cols(c)], in0=keep_all[:, cols(c)], in1=ci_sb[:, cols(c)], op=ALU.mult
-            )
 
-        def cell(c, z_t):
-            c_t = c_all[:, cols(c)]
-            nc.vector.scalar_tensor_tensor(
-                out=c_t, in0=z_t[:], scalar=m_f32[:], in1=i_all[:, cols(c)], op0=ALU.mult, op1=ALU.mult
-            )
-            nc.vector.tensor_tensor(out=c_t, in0=c_t, in1=keep_all[:, cols(c)], op=ALU.add)
-            nc.vector.tensor_tensor(out=c_times_n[:, cols(c)], in0=c_t, in1=n_all[:, cols(c)], op=ALU.mult)
-
-        def hidden(c, o_t):
-            h_t = h_all[:, cols(c)]
-            nc.vector.scalar_tensor_tensor(
-                out=h_t, in0=o_t[:], scalar=m_f32[:], in1=c_over_n[:, cols(c)], op0=ALU.mult, op1=ALU.mult
-            )
-            nc.vector.scalar_tensor_tensor(
-                out=h_t, in0=hi_sb[:, cols(c)], scalar=one_minus_m[:], in1=h_t, op0=ALU.mult, op1=ALU.add
-            )
-            nc.sync.dma_start(out=h_out[:, cols(c)], in_=h_t)
+        def kept_cell(c):
+            kept = keep_all[:, cols(c)]
+            nc.vector.tensor_tensor(out=kept, in0=kept, in1=ci_sb[:, cols(c)], op=ALU.mult)
 
         f_ts = {}
         for c in range(CHUNKS):
-            f_ts[c] = input_and_forget(c)
+            g_i = preactivation(GATE_I, c, work, "g_i")
+            g_f = preactivation(GATE_F, c, work, "g_f")
             if c > 0:
-                normaliser(c - 1, f_ts[c - 1])
+                normaliser_product(c - 1, f_ts[c - 1])
+            diff = work.tile([P, BANK], F32, tag="diff")
+            nc.vector.tensor_tensor(out=diff[:], in0=g_f[:], in1=g_i[:], op=ALU.subtract)
+            f_ts[c] = gate_exponentials(c, diff)
+            if c > 0:
+                normaliser_sum(c - 1)
+            nc.vector.tensor_tensor(out=m_all[:, cols(c)], in0=g_f[:], in1=g_i[:], op=ALU.max)
+            if c > 0:
+                kept_cell(c - 1)
             broadcast_bias(GATE_Z, c)
             broadcast_bias(GATE_O, c)
 
-        def finish(step):
-            gate, c = late_tiles[step]
-            if gate == GATE_Z:
-                cell(c, activated[step])
-            else:
-                hidden(c, activated[step])
+        def cell_product(c, z_t):
+            nc.vector.scalar_tensor_tensor(
+                out=c_all[:, cols(c)], in0=z_t[:], scalar=m_f32[:], in1=i_all[:, cols(c)],
+                op0=ALU.mult, op1=ALU.mult,
+            )
 
+        def cell_sum(c):
+            c_t = c_all[:, cols(c)]
+            nc.vector.tensor_tensor(out=c_t, in0=c_t, in1=keep_all[:, cols(c)], op=ALU.add)
+
+        def cell_times_n(c):
+            nc.vector.tensor_tensor(
+                out=c_times_n[:, cols(c)], in0=c_all[:, cols(c)], in1=n_all[:, cols(c)], op=ALU.mult
+            )
+
+        last = CHUNKS - 1
         activated = {}
         for step, (gate, c) in enumerate(late_tiles):
-            activated[step] = preactivation(gate, c, late, "late")
+            formed = step - LAG
             if step == 0:
-                normaliser(CHUNKS - 1, f_ts[CHUNKS - 1])
+                normaliser_product(last, f_ts[last])
+            if 0 <= formed <= last:
+                cell_product(formed, activated[formed])
+            activated[step] = preactivation(gate, c, late, "late")
             nc.scalar.activation(
                 out=activated[step][:], in_=activated[step][:],
                 func=(ACT.Tanh if gate == GATE_Z else ACT.Sigmoid),
             )
-            if (gate, c) == (GATE_Z, CHUNKS - 2):
+            if (gate, c) == (GATE_Z, last - 1):
                 nc.scalar.activation(out=inv_n_sq[:], in_=inv_n_sq[:], func=ACT.Ln)
-            if (gate, c) == (GATE_Z, CHUNKS - 1):
+            if (gate, c) == (GATE_Z, last):
                 nc.scalar.activation(out=inv_n_sq[:], in_=inv_n_sq[:], func=ACT.Exp, scale=-2.0)
                 nc.sync.dma_start(out=m_out, in_=m_all[:])
                 nc.sync.dma_start(out=n_out, in_=n_all[:])
-            if step >= LAG:
-                finish(step - LAG)
-            if step - LAG == CHUNKS - 1:
+            if step == 0:
+                normaliser_sum(last)
+                kept_cell(last)
+            if 0 <= formed <= last:
+                cell_sum(formed)
+            if formed == last:
                 nc.sync.dma_start(out=c_out, in_=c_all[:])
+            if 0 <= formed - 1 <= last:
+                cell_times_n(formed - 1)
+            if formed - 1 == last:
                 c_over_n = const.tile([P, D_H], F32, tag="i_then_c_over_n")
                 nc.vector.tensor_tensor(out=c_over_n[:], in0=c_times_n[:], in1=inv_n_sq[:], op=ALU.mult)
-        for step in range(len(late_tiles) - LAG, len(late_tiles)):
-            finish(step)
+
+        for first in range(0, CHUNKS, 2):
+            for c in (first, first + 1):
+                nc.vector.scalar_tensor_tensor(
+                    out=h_all[:, cols(c)], in0=activated[CHUNKS + c][:], scalar=m_f32[:],
+                    in1=c_over_n[:, cols(c)], op0=ALU.mult, op1=ALU.mult,
+                )
+            for c in (first, first + 1):
+                nc.vector.scalar_tensor_tensor(
+                    out=h_all[:, cols(c)], in0=hi_sb[:, cols(c)], scalar=one_minus_m[:],
+                    in1=h_all[:, cols(c)], op0=ALU.mult, op1=ALU.add,
+                )
+                nc.sync.dma_start(out=h_out[:, cols(c)], in_=h_all[:, cols(c)])

@@ -24,7 +24,7 @@ PSUM_BANKS = 8
 QUADRANTS = 4
 GATE_I, GATE_F, GATE_Z, GATE_O = 0, 1, 2, 3
 RING = 6
-SMALL_PER_TILE = 4
+SMALL_PER_TILE = 1
 LAG = 2
 
 FLOPS = 2 * P * (D_H + D_Z) * 4 * D_H
@@ -84,18 +84,18 @@ def tile_customlstmcell_w_kernel(
         ci_sb = const.tile([P, D_H], BF16)
         m_bf16 = const.tile([P, 1], BF16)
 
-        def scale_plane_loads(gate):
+        def scale_plane_loads(gate, word=I32):
             transfers = []
             for quad in range(QUADRANTS):
                 rows = slice(4 * quad, 4 * quad + 4)
                 live = slice(32 * quad, 32 * quad + 16)
                 transfers.append((
-                    h_planes[live, gate, :].bitcast(I32),
-                    w_scales[gate][:, rows, :].bitcast(I32),
+                    h_planes[live, gate, :].bitcast(word),
+                    w_scales[gate][:, rows, :].bitcast(word),
                 ))
                 transfers.append((
-                    z_planes[live, gate, :].bitcast(I32),
-                    r_scales[gate][0, rows, :].rearrange("r (c n) -> c r n", c=CHUNKS).bitcast(I32),
+                    z_planes[live, gate, :].bitcast(word),
+                    r_scales[gate][0, rows, :].rearrange("r (c n) -> c r n", c=CHUNKS).bitcast(word),
                 ))
             return transfers
 
@@ -110,13 +110,14 @@ def tile_customlstmcell_w_kernel(
             for destination, source in transfers:
                 nc.sync.dma_start(out=destination, in_=source)
 
-        waiting = (
+        waiting = [(ni_sb[:], Ni.flatten_outer_dims()), (ci_sb[:], Ci.flatten_outer_dims())]
+        for destination, source in (
             bias_row_loads(GATE_Z)
             + bias_row_loads(GATE_O)
-            + [(ni_sb[:], Ni.flatten_outer_dims()), (ci_sb[:], Ci.flatten_outer_dims())]
-            + scale_plane_loads(GATE_Z)
-            + scale_plane_loads(GATE_O)
-        )
+            + scale_plane_loads(GATE_Z, F32)
+            + scale_plane_loads(GATE_O, F32)
+        ):
+            nc.gpsimd.dma_start(out=destination, in_=source)
         weight_tiles = {}
 
         def load_weight_tile(index):

@@ -85,19 +85,20 @@ def tile_customlstmcell_w_kernel(
         m_bf16 = const.tile([P, 1], BF16)
 
         def scale_plane_loads(gate, word=I32):
-            transfers = []
+            h_transfers = []
+            z_transfers = []
             for quad in range(QUADRANTS):
                 rows = slice(4 * quad, 4 * quad + 4)
                 live = slice(32 * quad, 32 * quad + 16)
-                transfers.append((
+                h_transfers.append((
                     h_planes[live, gate, :].bitcast(word),
                     w_scales[gate][:, rows, :].bitcast(word),
                 ))
-                transfers.append((
+                z_transfers.append((
                     z_planes[live, gate, :].bitcast(word),
                     r_scales[gate][0, rows, :].rearrange("r (c n) -> c r n", c=CHUNKS).bitcast(word),
                 ))
-            return transfers
+            return h_transfers + z_transfers
 
         def bias_row_loads(gate):
             first = 32 * (gate % 2)
@@ -112,7 +113,8 @@ def tile_customlstmcell_w_kernel(
 
         waiting = [(ni_sb[:], Ni.flatten_outer_dims()), (ci_sb[:], Ci.flatten_outer_dims())]
         for destination, source in (
-            bias_row_loads(GATE_Z)
+            scale_plane_loads(GATE_F, F32)
+            + bias_row_loads(GATE_Z)
             + bias_row_loads(GATE_O)
             + scale_plane_loads(GATE_Z, F32)
             + scale_plane_loads(GATE_O, F32)
@@ -136,13 +138,15 @@ def tile_customlstmcell_w_kernel(
             if index >= 2:
                 load(waiting[SMALL_PER_TILE * (index - 2) : SMALL_PER_TILE * (index - 1)])
 
+        planes_i = scale_plane_loads(GATE_I)
         load([(hi_sb[:], Hi.flatten_outer_dims()), (zi_sb[:], Zi.flatten_outer_dims())])
+        load(planes_i[0:4])
         load_weight_tile(0)
-        load(scale_plane_loads(GATE_I))
-        load([(m_bf16[:], m.flatten_outer_dims())] + bias_row_loads(GATE_I) + bias_row_loads(GATE_F))
-        load_weight_tile(1)
+        load(bias_row_loads(GATE_I) + bias_row_loads(GATE_F))
         load([(mi_sb[:], Mi.flatten_outer_dims())])
-        load(scale_plane_loads(GATE_F))
+        load(planes_i[4:8])
+        load_weight_tile(1)
+        load([(m_bf16[:], m.flatten_outer_dims())])
         for index in range(2, RING):
             load_weight_tile(index)
 
@@ -196,14 +200,15 @@ def tile_customlstmcell_w_kernel(
 
         for c in range(CHUNKS):
             broadcast_bias(GATE_I, c)
-            broadcast_bias(GATE_F, c)
 
         m_f32 = const.tile([P, 1], F32)
-        nc.vector.tensor_copy(out=m_f32[:], in_=m_bf16[:])
         one_minus_m = const.tile([P, 1], F32)
-        nc.vector.tensor_scalar(
-            out=one_minus_m[:], in0=m_bf16[:], scalar1=-1.0, scalar2=1.0, op0=ALU.mult, op1=ALU.add
-        )
+
+        def blend_weights():
+            nc.vector.tensor_copy(out=m_f32[:], in_=m_bf16[:])
+            nc.vector.tensor_scalar(
+                out=one_minus_m[:], in0=m_bf16[:], scalar1=-1.0, scalar2=1.0, op0=ALU.mult, op1=ALU.add
+            )
 
         m_all = const.tile([P, D_H], F32)
         n_all = const.tile([P, D_H], F32)
@@ -267,6 +272,10 @@ def tile_customlstmcell_w_kernel(
         f_ts = {}
         for c in range(CHUNKS):
             g_i = preactivation(GATE_I, c, work, "g_i")
+            if c == 0:
+                for chunk in range(CHUNKS):
+                    broadcast_bias(GATE_F, chunk)
+                blend_weights()
             g_f = preactivation(GATE_F, c, work, "g_f")
             if c > 0:
                 normaliser_product(c - 1, f_ts[c - 1])

@@ -20,11 +20,11 @@ H_GROUPS = D_H // K_PASS
 GROUPS = H_GROUPS + D_Z // K_PASS
 BANK = 512
 CHUNKS = D_H // BANK
-PSUM_BANKS = 8
+ACC_BANKS = 6
+MISC_BANKS = 2
 QUADRANTS = 4
 GATE_I, GATE_F, GATE_Z, GATE_O = 0, 1, 2, 3
 RING = 6
-SMALL_PER_TILE = 1
 LAG = 2
 
 FLOPS = 2 * P * (D_H + D_Z) * 4 * D_H
@@ -48,7 +48,7 @@ def tile_customlstmcell_w_kernel(
     c_out, m_out, h_out, n_out = [o.flatten_outer_dims() for o in (out_0, out_1, out_2, out_3)]
 
     late_tiles = [(gate, c) for gate in (GATE_Z, GATE_O) for c in range(CHUNKS)]
-    tile_order = [(gate, c) for c in range(CHUNKS) for gate in (GATE_I, GATE_F)] + late_tiles
+    tile_order = [(GATE_I, g) for g in range(GROUPS)] + [(GATE_F, c) for c in range(CHUNKS)] + late_tiles
 
     def cols(c):
         return slice(BANK * c, BANK * (c + 1))
@@ -58,7 +58,8 @@ def tile_customlstmcell_w_kernel(
         ring = stack.enter_context(tc.tile_pool(name="ring", bufs=RING))
         work = stack.enter_context(tc.tile_pool(name="work", bufs=2))
         late = stack.enter_context(tc.tile_pool(name="late", bufs=CHUNKS))
-        psum = stack.enter_context(tc.psum_pool(name="psum", bufs=PSUM_BANKS))
+        acc_pool = stack.enter_context(tc.psum_pool(name="acc", bufs=ACC_BANKS))
+        misc_pool = stack.enter_context(tc.psum_pool(name="misc", bufs=MISC_BANKS))
         stack.enter_context(tc.manual_schedule())
 
         ident_f32 = const.tile([P, P], F32)
@@ -111,11 +112,8 @@ def tile_customlstmcell_w_kernel(
             for destination, source in transfers:
                 nc.sync.dma_start(out=destination, in_=source)
 
-        waiting = [(ni_sb[:], Ni.flatten_outer_dims()), (ci_sb[:], Ci.flatten_outer_dims())]
         for destination, source in (
             scale_plane_loads(GATE_F, F32)
-            + bias_row_loads(GATE_Z)
-            + bias_row_loads(GATE_O)
             + scale_plane_loads(GATE_Z, F32)
             + scale_plane_loads(GATE_O, F32)
         ):
@@ -124,8 +122,16 @@ def tile_customlstmcell_w_kernel(
 
         def load_weight_tile(index):
             gate, c = tile_order[index]
-            byte_cols = slice(4 * BANK * c, 4 * BANK * (c + 1))
             words = ring.tile([P, GROUPS, BANK], I32, tag="words", align_bytes=64)
+            weight_tiles[(gate, c)] = words
+            if gate == GATE_I:
+                group_words = w_words[gate][c] if c < H_GROUPS else r_words[gate][0]
+                nc.sync.dma_start(
+                    out=words[:, 0:CHUNKS, :].rearrange("p j n -> p (j n)"),
+                    in_=group_words.rearrange("p n t -> p (n t)").bitcast(I32),
+                )
+                return
+            byte_cols = slice(4 * BANK * c, 4 * BANK * (c + 1))
             nc.sync.dma_start(
                 out=words[:, 0:H_GROUPS, :],
                 in_=w_words[gate].rearrange("g p n t -> p g (n t)")[:, :, byte_cols].bitcast(I32),
@@ -134,21 +140,22 @@ def tile_customlstmcell_w_kernel(
                 out=words[:, H_GROUPS, :],
                 in_=r_words[gate].rearrange("g p n t -> p g (n t)")[:, 0, byte_cols].bitcast(I32),
             )
-            weight_tiles[(gate, c)] = words
-            if index >= 2:
-                load(waiting[SMALL_PER_TILE * (index - 2) : SMALL_PER_TILE * (index - 1)])
 
         planes_i = scale_plane_loads(GATE_I)
         load([(hi_sb[:], Hi.flatten_outer_dims()), (zi_sb[:], Zi.flatten_outer_dims())])
         load(planes_i[0:4])
         load_weight_tile(0)
         load(bias_row_loads(GATE_I) + bias_row_loads(GATE_F))
-        load([(mi_sb[:], Mi.flatten_outer_dims())])
-        load(planes_i[4:8])
         load_weight_tile(1)
+        load(planes_i[4:8])
+        load_weight_tile(2)
+        load(bias_row_loads(GATE_Z) + bias_row_loads(GATE_O))
+        load_weight_tile(3)
+        load([(mi_sb[:], Mi.flatten_outer_dims())])
+        load_weight_tile(4)
         load([(m_bf16[:], m.flatten_outer_dims())])
-        for index in range(2, RING):
-            load_weight_tile(index)
+        load_weight_tile(5)
+        load([(ni_sb[:], Ni.flatten_outer_dims()), (ci_sb[:], Ci.flatten_outer_dims())])
 
         x_bf16 = const.tile([P, GROUPS, P, 4], BF16, align_bytes=64)
         x_codes = const.tile([P, GROUPS, P], U32, align_bytes=64)
@@ -156,7 +163,7 @@ def tile_customlstmcell_w_kernel(
 
         def transpose_groups(source, first_group, n_groups):
             source_words = source.bitcast(F32)
-            halves = psum.tile([P, n_groups, 2, P], F32, tag="bank")
+            halves = misc_pool.tile([P, n_groups, 2, P], F32, tag="misc")
             for g in range(n_groups):
                 for u in range(2):
                     nc.tensor.transpose(
@@ -186,7 +193,7 @@ def tile_customlstmcell_w_kernel(
         bias = [const.tile([P, D_H], F32, name="bias%d" % gate) for gate in range(4)]
 
         def broadcast_bias(gate, c):
-            bank = psum.tile([P, BANK], F32, tag="bank")
+            bank = misc_pool.tile([P, BANK], F32, tag="misc")
             nc.tensor.matmul(
                 out=bank[:], lhsT=selector[:, gate % 2, :], rhs=bias_rows[gate // 2][:, cols(c)],
                 start=True, stop=True,
@@ -198,8 +205,6 @@ def tile_customlstmcell_w_kernel(
             else:
                 nc.scalar.copy(out=bias[gate][:, cols(c)], in_=bank[:])
 
-        for c in range(CHUNKS):
-            broadcast_bias(GATE_I, c)
 
         m_f32 = const.tile([P, 1], F32)
         one_minus_m = const.tile([P, 1], F32)
@@ -219,29 +224,48 @@ def tile_customlstmcell_w_kernel(
         inv_n_sq = const.tile([P, D_H], F32)
         c_times_n = const.tile([P, D_H], F32)
 
-        def preactivation(gate, c, pool, tag):
-            words = weight_tiles[(gate, c)]
-            acc = psum.tile([P, BANK], F32, tag="bank")
-            for g in range(GROUPS):
-                if g < H_GROUPS:
-                    plane = h_planes[4 * g : P, gate, cols(c)]
-                else:
-                    plane = z_planes[4 * c : P, gate, :]
-                nc.tensor.matmul_mx(
-                    out=acc[:],
-                    lhsT=x_codes[:, g, :].bitcast(FP8X4),
-                    lhsT_scale=x_scales[:, g, :],
-                    rhs=words[:, g, :].bitcast(FP8X4),
-                    rhs_scale=plane,
-                    start=(g == 0),
-                    stop=(g == GROUPS - 1),
-                )
-            follower = tile_order.index((gate, c)) + RING
+        def one_pass(acc, gate, c, g, words):
+            if g < H_GROUPS:
+                plane = h_planes[4 * g : P, gate, cols(c)]
+            else:
+                plane = z_planes[4 * c : P, gate, :]
+            nc.tensor.matmul_mx(
+                out=acc[:],
+                lhsT=x_codes[:, g, :].bitcast(FP8X4),
+                lhsT_scale=x_scales[:, g, :],
+                rhs=words.bitcast(FP8X4),
+                rhs_scale=plane,
+                start=(g == 0),
+                stop=(g == GROUPS - 1),
+            )
+
+        def load_follower(tile):
+            follower = tile_order.index(tile) + RING
             if follower < len(tile_order):
                 load_weight_tile(follower)
-            pre = pool.tile([P, BANK], F32, tag=tag)
-            nc.vector.tensor_tensor(out=pre[:], in0=acc[:], in1=bias[gate][:, cols(c)], op=ALU.add)
-            return pre
+
+        def gate_sums(gate, between):
+            accs = []
+            for c in range(CHUNKS):
+                acc = acc_pool.tile([P, BANK], F32, tag="acc", name="acc%d" % c)
+                accs.append(acc)
+            for g in range(GROUPS):
+                for c in range(CHUNKS):
+                    one_pass(accs[c], gate, c, g, weight_tiles[(gate, g)][:, c, :])
+                load_follower((gate, g))
+                if g in between:
+                    between[g]()
+            return accs
+
+        def chunk_sums(gate, c):
+            acc = acc_pool.tile([P, BANK], F32, tag="acc")
+            for g in range(GROUPS):
+                one_pass(acc, gate, c, g, weight_tiles[(gate, c)][:, g, :])
+            load_follower((gate, c))
+            return acc
+
+        def preactivation(gate, c, acc, out):
+            nc.vector.tensor_tensor(out=out, in0=acc[:], in1=bias[gate][:, cols(c)], op=ALU.add)
 
 
         def gate_exponentials(c, diff):
@@ -269,26 +293,31 @@ def tile_customlstmcell_w_kernel(
             kept = keep_all[:, cols(c)]
             nc.vector.tensor_tensor(out=kept, in0=kept, in1=ci_sb[:, cols(c)], op=ALU.mult)
 
+        def spread(gate):
+            for chunk in range(CHUNKS):
+                broadcast_bias(gate, chunk)
+
+        i_sums = gate_sums(GATE_I, {
+            0: lambda: spread(GATE_I), 2: lambda: spread(GATE_Z), 3: lambda: spread(GATE_O), 4: lambda: spread(GATE_F),
+        })
+        blend_weights()
+        for c in range(CHUNKS):
+            preactivation(GATE_I, c, i_sums[c], m_all[:, cols(c)])
+
         f_ts = {}
         for c in range(CHUNKS):
-            g_i = preactivation(GATE_I, c, work, "g_i")
-            if c == 0:
-                for chunk in range(CHUNKS):
-                    broadcast_bias(GATE_F, chunk)
-                blend_weights()
-            g_f = preactivation(GATE_F, c, work, "g_f")
+            g_f = work.tile([P, BANK], F32, tag="g_f")
+            preactivation(GATE_F, c, chunk_sums(GATE_F, c), g_f[:])
             if c > 0:
                 normaliser_product(c - 1, f_ts[c - 1])
             diff = work.tile([P, BANK], F32, tag="diff")
-            nc.vector.tensor_tensor(out=diff[:], in0=g_f[:], in1=g_i[:], op=ALU.subtract)
+            nc.vector.tensor_tensor(out=diff[:], in0=g_f[:], in1=m_all[:, cols(c)], op=ALU.subtract)
             f_ts[c] = gate_exponentials(c, diff)
             if c > 0:
                 normaliser_sum(c - 1)
-            nc.vector.tensor_tensor(out=m_all[:, cols(c)], in0=g_f[:], in1=g_i[:], op=ALU.max)
+            nc.vector.tensor_tensor(out=m_all[:, cols(c)], in0=g_f[:], in1=m_all[:, cols(c)], op=ALU.max)
             if c > 0:
                 kept_cell(c - 1)
-            broadcast_bias(GATE_Z, c)
-            broadcast_bias(GATE_O, c)
 
         def cell_product(c, z_t):
             nc.vector.scalar_tensor_tensor(
@@ -313,7 +342,8 @@ def tile_customlstmcell_w_kernel(
                 normaliser_product(last, f_ts[last])
             if 0 <= formed <= last:
                 cell_product(formed, activated[formed])
-            activated[step] = preactivation(gate, c, late, "late")
+            activated[step] = late.tile([P, BANK], F32, tag="late", name="activated")
+            preactivation(gate, c, chunk_sums(gate, c), activated[step][:])
             nc.scalar.activation(
                 out=activated[step][:], in_=activated[step][:],
                 func=(ACT.Tanh if gate == GATE_Z else ACT.Sigmoid),

@@ -216,6 +216,7 @@ def tile_customlstmcell_w_kernel(
             )
 
         m_all = const.tile([P, D_H], F32)
+        diff_all = const.tile([P, D_H], F32)
         n_all = const.tile([P, D_H], F32)
         c_all = const.tile([P, D_H], F32)
         h_all = const.tile([P, D_H], F32)
@@ -271,9 +272,9 @@ def tile_customlstmcell_w_kernel(
         def gate_exponentials(c, diff):
             f_t = work.tile([P, BANK], F32, tag="f_t")
             i_t = i_all[:, cols(c)]
-            nc.scalar.activation(out=f_t[:], in_=diff[:], func=ACT.Relu, scale=-1.0)
-            nc.scalar.activation(out=i_t, in_=diff[:], func=ACT.Relu)
-            nc.scalar.activation(out=f_t[:], in_=f_t[:], func=ACT.Exp, scale=-1.0)
+            nc.vector.tensor_scalar_min(out=f_t[:], in0=diff, scalar1=0.0)
+            nc.scalar.activation(out=i_t, in_=diff, func=ACT.Relu)
+            nc.scalar.activation(out=f_t[:], in_=f_t[:], func=ACT.Exp)
             nc.scalar.activation(out=i_t, in_=i_t, func=ACT.Exp, scale=-1.0)
             nc.scalar.activation(
                 out=keep_all[:, cols(c)], in_=f_t[:], func=ACT.Identity,
@@ -301,22 +302,27 @@ def tile_customlstmcell_w_kernel(
             0: lambda: spread(GATE_I), 2: lambda: spread(GATE_Z), 3: lambda: spread(GATE_O), 4: lambda: spread(GATE_F),
         })
         blend_weights()
-        for c in range(CHUNKS):
-            preactivation(GATE_I, c, i_sums[c], m_all[:, cols(c)])
+        for c in range(CHUNKS + 1):
+            if c < CHUNKS:
+                preactivation(GATE_I, c, i_sums[c], m_all[:, cols(c)])
+            if c > 0:
+                w = cols(c - 1)
+                nc.vector.tensor_tensor(out=diff_all[:, w], in0=bias[GATE_F][:, w], in1=m_all[:, w], op=ALU.subtract)
 
         f_ts = {}
         for c in range(CHUNKS):
-            g_f = work.tile([P, BANK], F32, tag="g_f")
-            preactivation(GATE_F, c, chunk_sums(GATE_F, c), g_f[:])
+            w = cols(c)
+            nc.vector.tensor_tensor(
+                out=diff_all[:, w], in0=chunk_sums(GATE_F, c)[:], in1=diff_all[:, w], op=ALU.add
+            )
             if c > 0:
                 normaliser_product(c - 1, f_ts[c - 1])
-            diff = work.tile([P, BANK], F32, tag="diff")
-            nc.vector.tensor_tensor(out=diff[:], in0=g_f[:], in1=m_all[:, cols(c)], op=ALU.subtract)
-            f_ts[c] = gate_exponentials(c, diff)
+            f_ts[c] = gate_exponentials(c, diff_all[:, w])
+            nc.vector.scalar_tensor_tensor(
+                out=m_all[:, w], in0=diff_all[:, w], scalar=0.0, in1=m_all[:, w], op0=ALU.max, op1=ALU.add
+            )
             if c > 0:
                 normaliser_sum(c - 1)
-            nc.vector.tensor_tensor(out=m_all[:, cols(c)], in0=g_f[:], in1=m_all[:, cols(c)], op=ALU.max)
-            if c > 0:
                 kept_cell(c - 1)
 
         def cell_product(c, z_t):

from contextlib import ExitStack

import concourse.mybir as mybir
from concourse.masks import make_identity

F32 = mybir.dt.float32
BF16 = mybir.dt.bfloat16
I32 = mybir.dt.int32
U32 = mybir.dt.uint32
U8 = mybir.dt.uint8
FP8X4 = mybir.dt.float8_e4m3fn_x4
ALU = mybir.AluOpType
ACT = mybir.ActivationFunctionType

P = 128
D_H = 2048
D_Z = 512
K_PASS = 512
H_GROUPS = D_H // K_PASS
GROUPS = H_GROUPS + D_Z // K_PASS
BANK = 512
CHUNKS = D_H // BANK
ACC_BANKS = 6
MISC_BANKS = 2
QUADRANTS = 4
GATE_I, GATE_F, GATE_Z, GATE_O = 0, 1, 2, 3
RING = 6
LAG = 2

FLOPS = 2 * P * (D_H + D_Z) * 4 * D_H


def tile_customlstmcell_w_kernel(
    tc, Zi, Ci, Mi, Hi, Ni, m,
    WI_w_words, WI_w_scales, WI_b, WF_w_words, WF_w_scales, WF_b,
    WO_w_words, WO_w_scales, WO_b, WZ_w_words, WZ_w_scales, WZ_b,
    RI_w_words, RI_w_scales, RI_b, RF_w_words, RF_w_scales, RF_b,
    RO_w_words, RO_w_scales, RO_b, RZ_w_words, RZ_w_scales, RZ_b,
    out_0, out_1, out_2, out_3,
):
    nc = tc.nc
    w_words = [WI_w_words, WF_w_words, WZ_w_words, WO_w_words]
    w_scales = [WI_w_scales, WF_w_scales, WZ_w_scales, WO_w_scales]
    w_bias = [WI_b, WF_b, WZ_b, WO_b]
    r_words = [RI_w_words, RF_w_words, RZ_w_words, RO_w_words]
    r_scales = [RI_w_scales, RF_w_scales, RZ_w_scales, RO_w_scales]
    r_bias = [RI_b, RF_b, RZ_b, RO_b]
    c_out, m_out, h_out, n_out = [o.flatten_outer_dims() for o in (out_0, out_1, out_2, out_3)]

    late_tiles = [(gate, c) for gate in (GATE_Z, GATE_O) for c in range(CHUNKS)]
    tile_order = [(GATE_I, g) for g in range(GROUPS)] + [(GATE_F, c) for c in range(CHUNKS)] + late_tiles

    def cols(c):
        return slice(BANK * c, BANK * (c + 1))

    with ExitStack() as stack:
        const = stack.enter_context(tc.tile_pool(name="const", bufs=1))
        ring = stack.enter_context(tc.tile_pool(name="ring", bufs=RING))
        work = stack.enter_context(tc.tile_pool(name="work", bufs=2))
        late = stack.enter_context(tc.tile_pool(name="late", bufs=CHUNKS))
        acc_pool = stack.enter_context(tc.psum_pool(name="acc", bufs=ACC_BANKS))
        misc_pool = stack.enter_context(tc.psum_pool(name="misc", bufs=MISC_BANKS))
        stack.enter_context(tc.manual_schedule())

        ident_f32 = const.tile([P, P], F32)
        make_identity(nc, ident_f32[:])

        h_planes = const.tile([P, 4, D_H], U8, align_bytes=64)
        nc.vector.memset(h_planes[:].bitcast(I32), 0)
        z_planes = const.tile([P, 4, BANK], U8, align_bytes=64)
        nc.vector.memset(z_planes[:].bitcast(I32), 0)

        bias_rows = [const.tile([P, D_H], BF16, name="bias_rows%d" % pair) for pair in range(2)]
        for pair in range(2):
            nc.vector.memset(bias_rows[pair][:], 0.0)
        selector = const.tile([P, 2, P], BF16)
        nc.vector.memset(selector[:], 0.0)
        for second in range(2):
            nc.vector.memset(selector[32 * second : 32 * second + 32, second, :], 1.0)

        hi_sb = const.tile([P, D_H], BF16)
        zi_sb = const.tile([P, D_Z], BF16)
        mi_sb = const.tile([P, D_H], BF16)
        ni_sb = const.tile([P, D_H], BF16)
        ci_sb = const.tile([P, D_H], BF16)
        m_bf16 = const.tile([P, 1], BF16)

        def scale_plane_loads(gate, word=I32):
            h_transfers = []
            z_transfers = []
            for quad in range(QUADRANTS):
                rows = slice(4 * quad, 4 * quad + 4)
                live = slice(32 * quad, 32 * quad + 16)
                h_transfers.append((
                    h_planes[live, gate, :].bitcast(word),
                    w_scales[gate][:, rows, :].bitcast(word),
                ))
                z_transfers.append((
                    z_planes[live, gate, :].bitcast(word),
                    r_scales[gate][0, rows, :].rearrange("r (c n) -> c r n", c=CHUNKS).bitcast(word),
                ))
            return h_transfers + z_transfers

        def bias_row_loads(gate):
            first = 32 * (gate % 2)
            return [
                (bias_rows[gate // 2][row : row + 1, :], vector.rearrange("(o n) -> o n", o=1))
                for row, vector in ((first, w_bias[gate]), (first + 1, r_bias[gate]))
            ]

        def load(transfers):
            for destination, source in transfers:
                nc.sync.dma_start(out=destination, in_=source)

        for destination, source in (
            scale_plane_loads(GATE_F, F32)
            + scale_plane_loads(GATE_Z, F32)
            + scale_plane_loads(GATE_O, F32)
        ):
            nc.gpsimd.dma_start(out=destination, in_=source)
        weight_tiles = {}

        def load_weight_tile(index):
            gate, c = tile_order[index]
            words = ring.tile([P, GROUPS, BANK], I32, tag="words", align_bytes=64)
            weight_tiles[(gate, c)] = words
            if gate == GATE_I:
                group_words = w_words[gate][c] if c < H_GROUPS else r_words[gate][0]
                nc.sync.dma_start(
                    out=words[:, 0:CHUNKS, :].rearrange("p j n -> p (j n)"),
                    in_=group_words.rearrange("p n t -> p (n t)").bitcast(I32),
                )
                return
            byte_cols = slice(4 * BANK * c, 4 * BANK * (c + 1))
            nc.sync.dma_start(
                out=words[:, 0:H_GROUPS, :],
                in_=w_words[gate].rearrange("g p n t -> p g (n t)")[:, :, byte_cols].bitcast(I32),
            )
            nc.sync.dma_start(
                out=words[:, H_GROUPS, :],
                in_=r_words[gate].rearrange("g p n t -> p g (n t)")[:, 0, byte_cols].bitcast(I32),
            )

        planes_i = scale_plane_loads(GATE_I)
        load([(hi_sb[:], Hi.flatten_outer_dims()), (zi_sb[:], Zi.flatten_outer_dims())])
        load(planes_i[0:4])
        load_weight_tile(0)
        load(bias_row_loads(GATE_I) + bias_row_loads(GATE_F))
        load_weight_tile(1)
        load(planes_i[4:8])
        load_weight_tile(2)
        load(bias_row_loads(GATE_Z) + bias_row_loads(GATE_O))
        load_weight_tile(3)
        load([(mi_sb[:], Mi.flatten_outer_dims())])
        load_weight_tile(4)
        load([(m_bf16[:], m.flatten_outer_dims())])
        load_weight_tile(5)
        load([(ni_sb[:], Ni.flatten_outer_dims()), (ci_sb[:], Ci.flatten_outer_dims())])

        x_bf16 = const.tile([P, GROUPS, P, 4], BF16, align_bytes=64)
        x_codes = const.tile([P, GROUPS, P], U32, align_bytes=64)
        x_scales = const.tile([P, GROUPS, P], U8, align_bytes=64)

        def transpose_groups(source, first_group, n_groups):
            source_words = source.bitcast(F32)
            halves = misc_pool.tile([P, n_groups, 2, P], F32, tag="misc")
            for g in range(n_groups):
                for u in range(2):
                    nc.tensor.transpose(
                        halves[:, g, u, :],
                        source_words[:, 256 * g + u : 256 * (g + 1) : 2],
                        ident_f32[:],
                    )
            nc.vector.tensor_copy(
                out=x_bf16[:, first_group : first_group + n_groups].bitcast(F32),
                in_=halves[:].rearrange("p g u r -> p g r u"),
            )

        def quantise_groups(first_group, n_groups):
            groups = slice(first_group, first_group + n_groups)
            nc.vector.quantize_mx(
                out=x_codes[:, groups, :].rearrange("p g r -> p (g r)").bitcast(FP8X4),
                scales=x_scales[:, groups, :].rearrange("p g r -> p (g r)"),
                in_=x_bf16[:, groups].rearrange("p g r t -> p (g r t)"),
            )

        transpose_groups(hi_sb[:, 0 : 2 * K_PASS], 0, 2)
        transpose_groups(hi_sb[:, 2 * K_PASS : 4 * K_PASS], 2, 2)
        transpose_groups(zi_sb[:], H_GROUPS, 1)
        quantise_groups(0, H_GROUPS)
        quantise_groups(H_GROUPS, 1)

        bias = [const.tile([P, D_H], F32, name="bias%d" % gate) for gate in range(4)]

        def broadcast_bias(gate, c):
            bank = misc_pool.tile([P, BANK], F32, tag="misc")
            nc.tensor.matmul(
                out=bank[:], lhsT=selector[:, gate % 2, :], rhs=bias_rows[gate // 2][:, cols(c)],
                start=True, stop=True,
            )
            if gate == GATE_F:
                nc.vector.tensor_tensor(
                    out=bias[gate][:, cols(c)], in0=bank[:], in1=mi_sb[:, cols(c)], op=ALU.add
                )
            else:
                nc.scalar.copy(out=bias[gate][:, cols(c)], in_=bank[:])


        m_f32 = const.tile([P, 1], F32)
        one_minus_m = const.tile([P, 1], F32)

        def blend_weights():
            nc.vector.tensor_copy(out=m_f32[:], in_=m_bf16[:])
            nc.vector.tensor_scalar(
                out=one_minus_m[:], in0=m_bf16[:], scalar1=-1.0, scalar2=1.0, op0=ALU.mult, op1=ALU.add
            )

        m_all = const.tile([P, D_H], F32)
        diff_all = const.tile([P, D_H], F32)
        n_all = const.tile([P, D_H], F32)
        c_all = const.tile([P, D_H], F32)
        h_all = const.tile([P, D_H], F32)
        i_all = const.tile([P, D_H], F32, tag="i_then_c_over_n")
        keep_all = const.tile([P, D_H], F32)
        inv_n_sq = const.tile([P, D_H], F32)
        c_times_n = const.tile([P, D_H], F32)

        def one_pass(acc, gate, c, g, words):
            if g < H_GROUPS:
                plane = h_planes[4 * g : P, gate, cols(c)]
            else:
                plane = z_planes[4 * c : P, gate, :]
            nc.tensor.matmul_mx(
                out=acc[:],
                lhsT=x_codes[:, g, :].bitcast(FP8X4),
                lhsT_scale=x_scales[:, g, :],
                rhs=words.bitcast(FP8X4),
                rhs_scale=plane,
                start=(g == 0),
                stop=(g == GROUPS - 1),
            )

        def load_follower(tile):
            follower = tile_order.index(tile) + RING
            if follower < len(tile_order):
                load_weight_tile(follower)

        def gate_sums(gate, between):
            accs = []
            for c in range(CHUNKS):
                acc = acc_pool.tile([P, BANK], F32, tag="acc", name="acc%d" % c)
                accs.append(acc)
            for g in range(GROUPS):
                for c in range(CHUNKS):
                    one_pass(accs[c], gate, c, g, weight_tiles[(gate, g)][:, c, :])
                load_follower((gate, g))
                if g in between:
                    between[g]()
            return accs

        def chunk_sums(gate, c):
            acc = acc_pool.tile([P, BANK], F32, tag="acc")
            for g in range(GROUPS):
                one_pass(acc, gate, c, g, weight_tiles[(gate, c)][:, g, :])
            load_follower((gate, c))
            return acc

        def preactivation(gate, c, acc, out):
            nc.vector.tensor_tensor(out=out, in0=acc[:], in1=bias[gate][:, cols(c)], op=ALU.add)


        def gate_exponentials(c, diff):
            f_t = work.tile([P, BANK], F32, tag="f_t")
            i_t = i_all[:, cols(c)]
            nc.vector.tensor_scalar_min(out=f_t[:], in0=diff, scalar1=0.0)
            nc.scalar.activation(out=i_t, in_=diff, func=ACT.Relu)
            nc.scalar.activation(out=f_t[:], in_=f_t[:], func=ACT.Exp)
            nc.scalar.activation(out=i_t, in_=i_t, func=ACT.Exp, scale=-1.0)
            nc.scalar.activation(
                out=keep_all[:, cols(c)], in_=f_t[:], func=ACT.Identity,
                scale=m_f32[:], bias=one_minus_m[:],
            )
            return f_t

        def normaliser_product(c, f_t):
            nc.vector.tensor_tensor(out=n_all[:, cols(c)], in0=f_t[:], in1=ni_sb[:, cols(c)], op=ALU.mult)

        def normaliser_sum(c):
            n_t = n_all[:, cols(c)]
            nc.vector.tensor_tensor(out=n_t, in0=n_t, in1=i_all[:, cols(c)], op=ALU.add)
            nc.scalar.activation(out=inv_n_sq[:, cols(c)], in_=n_t, func=ACT.Abs)

        def kept_cell(c):
            kept = keep_all[:, cols(c)]
            nc.vector.tensor_tensor(out=kept, in0=kept, in1=ci_sb[:, cols(c)], op=ALU.mult)

        def spread(gate):
            for chunk in range(CHUNKS):
                broadcast_bias(gate, chunk)

        i_sums = gate_sums(GATE_I, {
            0: lambda: spread(GATE_I), 2: lambda: spread(GATE_Z), 3: lambda: spread(GATE_O), 4: lambda: spread(GATE_F),
        })
        blend_weights()
        for c in range(CHUNKS + 1):
            if c < CHUNKS:
                preactivation(GATE_I, c, i_sums[c], m_all[:, cols(c)])
            if c > 0:
                w = cols(c - 1)
                nc.vector.tensor_tensor(out=diff_all[:, w], in0=bias[GATE_F][:, w], in1=m_all[:, w], op=ALU.subtract)

        f_ts = {}
        for c in range(CHUNKS):
            w = cols(c)
            nc.vector.tensor_tensor(
                out=diff_all[:, w], in0=chunk_sums(GATE_F, c)[:], in1=diff_all[:, w], op=ALU.add
            )
            if c > 0:
                normaliser_product(c - 1, f_ts[c - 1])
            f_ts[c] = gate_exponentials(c, diff_all[:, w])
            nc.vector.scalar_tensor_tensor(
                out=m_all[:, w], in0=diff_all[:, w], scalar=0.0, in1=m_all[:, w], op0=ALU.max, op1=ALU.add
            )
            if c > 0:
                normaliser_sum(c - 1)
                kept_cell(c - 1)

        def cell_product(c, z_t):
            nc.vector.scalar_tensor_tensor(
                out=c_all[:, cols(c)], in0=z_t[:], scalar=m_f32[:], in1=i_all[:, cols(c)],
                op0=ALU.mult, op1=ALU.mult,
            )

        def cell_sum(c):
            c_t = c_all[:, cols(c)]
            nc.vector.tensor_tensor(out=c_t, in0=c_t, in1=keep_all[:, cols(c)], op=ALU.add)

        def cell_times_n(c):
            nc.vector.tensor_tensor(
                out=c_times_n[:, cols(c)], in0=c_all[:, cols(c)], in1=n_all[:, cols(c)], op=ALU.mult
            )

        last = CHUNKS - 1
        activated = {}
        for step, (gate, c) in enumerate(late_tiles):
            formed = step - LAG
            if step == 0:
                normaliser_product(last, f_ts[last])
            if 0 <= formed <= last:
                cell_product(formed, activated[formed])
            activated[step] = late.tile([P, BANK], F32, tag="late", name="activated")
            preactivation(gate, c, chunk_sums(gate, c), activated[step][:])
            nc.scalar.activation(
                out=activated[step][:], in_=activated[step][:],
                func=(ACT.Tanh if gate == GATE_Z else ACT.Sigmoid),
            )
            if (gate, c) == (GATE_Z, last - 1):
                nc.scalar.activation(out=inv_n_sq[:], in_=inv_n_sq[:], func=ACT.Ln)
            if (gate, c) == (GATE_Z, last):
                nc.scalar.activation(out=inv_n_sq[:], in_=inv_n_sq[:], func=ACT.Exp, scale=-2.0)
                nc.sync.dma_start(out=m_out, in_=m_all[:])
                nc.sync.dma_start(out=n_out, in_=n_all[:])
            if step == 0:
                normaliser_sum(last)
                kept_cell(last)
            if 0 <= formed <= last:
                cell_sum(formed)
            if formed == last:
                nc.sync.dma_start(out=c_out, in_=c_all[:])
            if 0 <= formed - 1 <= last:
                cell_times_n(formed - 1)
            if formed - 1 == last:
                c_over_n = const.tile([P, D_H], F32, tag="i_then_c_over_n")
                nc.vector.tensor_tensor(out=c_over_n[:], in0=c_times_n[:], in1=inv_n_sq[:], op=ALU.mult)

        for first in range(0, CHUNKS, 2):
            for c in (first, first + 1):
                nc.vector.scalar_tensor_tensor(
                    out=h_all[:, cols(c)], in0=activated[CHUNKS + c][:], scalar=m_f32[:],
                    in1=c_over_n[:, cols(c)], op0=ALU.mult, op1=ALU.mult,
                )
            for c in (first, first + 1):
                nc.vector.scalar_tensor_tensor(
                    out=h_all[:, cols(c)], in0=hi_sb[:, cols(c)], scalar=one_minus_m[:],
                    in1=h_all[:, cols(c)], op0=ALU.mult, op1=ALU.add,
                )
                nc.sync.dma_start(out=h_out[:, cols(c)], in_=h_all[:, cols(c)])
